import numpy as np
import ml_dtypes


def mxq(x, axis, fmt="e4m3"):
    dtype, down = {"e4m3": (ml_dtypes.float8_e4m3fn, 7), "e5m2": (ml_dtypes.float8_e5m2, 14)}[fmt]
    v = np.moveaxis(np.asarray(x, np.float32).astype(ml_dtypes.bfloat16).astype(np.float64), axis, -1)
    blocks = v.reshape(v.shape[:-1] + (-1, 32))
    amax = np.abs(blocks).max(-1, keepdims=True)
    byte = np.maximum(np.where(amax > 0, np.frexp(amax)[1] - 1 + 127, 0) - down, 1)
    scale = np.exp2(byte - 127.0)
    codes = (blocks / scale).astype(np.float32).astype(dtype).astype(np.float64)
    return np.moveaxis((codes * scale).reshape(v.shape), -1, axis)


WIDE = False


def mx_kscale(k):
    if not WIDE:
        return np.ones(k)
    levels = np.array([10, -10, 5, -5, 0])
    a = np.random.permutation(np.resize(levels, k // 512 * 4)).reshape(k // 512, 4)
    idx = np.arange(k)
    return np.exp2(a[idx // 512, idx % 128 // 32])


BF16 = ml_dtypes.bfloat16


def bf(x):
    return np.asarray(x, np.float32).astype(BF16)


def f64(x):
    return np.asarray(x).astype(np.float64)


B, E, D = 256, 2048, 2048


def hard_sigmoid(z):
    return np.clip(z / 6.0 + 0.5, 0.0, 1.0)


def setup_inputs():
    s = mx_kscale(E)
    t = mx_kscale(D)
    return {
        "x": bf(np.random.standard_normal((B, E)) * s),
        "state_x": bf(np.random.standard_normal((B, E)) * s),
        "time_mix_r": bf(np.random.uniform(0.0, 1.0, (1, E))),
        "W_receptance": bf(np.random.standard_normal((D, E)) * 3.5 / np.sqrt(E) / s[None, :]),
        "wkv_num": bf((0.5 + 0.5 * np.random.standard_normal((B, D))) * t),
        "wkv_den": bf(0.5 + 1.5 * np.random.uniform(0.0, 1.0, (B, D))),
        "W_output": bf(np.random.standard_normal((E, D)) * 2.0 / np.sqrt(D) / t[None, :]),
    }


def reference(x, state_x, time_mix_r, W_receptance, wkv_num, wkv_den, W_output):
    x, state_x, mr = f64(x), f64(state_x), f64(time_mix_r)
    xr = x * mr + state_x * (1.0 - mr)
    r = hard_sigmoid(mxq(xr, 1, "e4m3") @ mxq(f64(W_receptance), 1, "e4m3").T)
    h = r * f64(wkv_num) / f64(wkv_den)
    return mxq(h, 1, "e4m3") @ mxq(f64(W_output), 1, "e4m3").T

@@ -1,0 +1,264 @@
+from contextlib import ExitStack
+
+import concourse.mybir as mybir
+from concourse.masks import make_identity
+
+F32 = mybir.dt.float32
+BF16 = mybir.dt.bfloat16
+U32 = mybir.dt.uint32
+U8 = mybir.dt.uint8
+FP8X4 = mybir.dt.float8_e4m3fn_x4
+ACT = mybir.ActivationFunctionType
+ALU = mybir.AluOpType
+
+P = 128
+B = 256
+K = 2048
+PACK = 4
+PASSES = K // (P * PACK)
+SLAB = 2 * P
+SLABS = K // SLAB
+RAW_BUFS = 8
+AHEAD = 2
+
+FLOPS = 2 * 2 * B * K * K
+
+
+def tile_rwkv_timemix_for_quant_pb_kernel(
+    tc, x, state_x, time_mix_r, W_receptance, wkv_num, wkv_den, W_output, out
+):
+    nc = tc.nc
+    with ExitStack() as ctx:
+        consts = ctx.enter_context(tc.tile_pool(name="consts", bufs=1))
+        acts = ctx.enter_context(tc.tile_pool(name="acts", bufs=1))
+        raw = ctx.enter_context(tc.tile_pool(name="raw", bufs=RAW_BUFS))
+        stage = ctx.enter_context(tc.tile_pool(name="stage", bufs=3))
+        quantised = ctx.enter_context(tc.tile_pool(name="quantised", bufs=AHEAD + 2))
+        keep = ctx.enter_context(tc.tile_pool(name="keep", bufs=1))
+        work = ctx.enter_context(tc.tile_pool(name="work", bufs=2))
+        tbanks = ctx.enter_context(tc.psum_pool(name="tbanks", bufs=6))
+        sums = ctx.enter_context(tc.psum_pool(name="sums", bufs=2))
+        ctx.enter_context(tc.manual_schedule())
+
+        ident = consts.tile([P, P], F32)
+        make_identity(nc, ident[:])
+
+        mix_rows = consts.tile([P, 2 * P], BF16)
+        nc.vector.memset(mix_rows[:], 0.0)
+        nc.sync.dma_start(
+            out=mix_rows[0 : 2 * PASSES, :],
+            in_=time_mix_r.rearrange("o (w c) -> (o w) c", w=2 * PASSES),
+        )
+
+        def load_rows(dst, rows):
+            nc.sync.dma_start(out=dst[:], in_=rows.rearrange("(p s) k -> p s k", s=2))
+
+        x_raw = acts.tile([P, 2, K], BF16)
+        load_rows(x_raw, x)
+        sx_raw = acts.tile([P, 2, K], BF16)
+        load_rows(sx_raw, state_x)
+        den_raw = acts.tile([P, 2, K], BF16)
+        load_rows(den_raw, wkv_den)
+        num_raw = acts.tile([P, 2, K], BF16)
+        load_rows(num_raw, wkv_num)
+
+        slab_raw = {}
+
+        def load_slab(i):
+            w_raw = raw.tile([P, 2, K], BF16)
+            weight = W_receptance if i < SLABS else W_output
+            c = i % SLABS
+            load_rows(w_raw, weight[c * SLAB : (c + 1) * SLAB, :])
+            slab_raw[i] = w_raw
+
+        for i in range(RAW_BUFS):
+            load_slab(i)
+
+        def transpose_pass(src, g):
+            words = src[:].bitcast(F32)
+            bank = tbanks.tile([P, 2, SLAB], F32)
+            for u in range(2):
+                w = 2 * g + u
+                for s in range(2):
+                    nc.tensor.transpose(
+                        bank[:, u, s * P : (s + 1) * P], words[:, s, w * P : (w + 1) * P], ident[:]
+                    )
+            return bank
+
+        def values(bank):
+            return bank[:].bitcast(BF16).rearrange("p u (j e) -> p j u e", e=2)
+
+        def by_pairs(ap):
+            return ap.rearrange("p j (u e) -> p j u e", e=2)
+
+        mix_bank = tbanks.tile([P, 2, SLAB], F32, tag="bank")
+        nc.tensor.transpose(mix_bank[:, 0, 0:P], mix_rows[:].bitcast(F32), ident[:])
+        mix = consts.tile([P, PACK * PASSES], F32)
+        nc.vector.tensor_copy(out=mix[:], in_=mix_bank[:, 0, 0 : 2 * PASSES].bitcast(BF16))
+        one_minus_mix = consts.tile([P, PACK * PASSES], F32)
+        nc.vector.tensor_scalar(
+            out=one_minus_mix[:], in0=mix[:], scalar1=-1.0, scalar2=1.0, op0=ALU.mult, op1=ALU.add
+        )
+
+        xr_codes = keep.tile([P, PASSES, B], U32, align_bytes=64)
+        xr_scales = keep.tile([P, PASSES, B], U8, align_bytes=64)
+        h_codes = keep.tile([P, PASSES, B], U32, align_bytes=64)
+        h_scales = keep.tile([P, PASSES, B], U8, align_bytes=64)
+
+        def quantise_pass(grouped, codes, scales, g):
+            nc.vector.quantize_mx(
+                out=codes[:, g, :].bitcast(FP8X4),
+                scales=scales[:, g, :],
+                in_=grouped[:].rearrange("p j t -> p (j t)"),
+            )
+
+        x_banks = [transpose_pass(x_raw, g) for g in range(PASSES)]
+        xr_grouped = {}
+        for g in range(PASSES):
+            x_vals = values(x_banks[g])
+            sx_vals = values(transpose_pass(sx_raw, g))
+            sx_part = work.tile([P, PACK, B], F32)
+            xr_rows = work.tile([P, PACK, B], BF16)
+            for u in range(2):
+                for e in range(2):
+                    t = 2 * u + e
+                    nc.scalar.activation(
+                        out=sx_part[:, t, :],
+                        in_=sx_vals[:, :, u, e],
+                        func=ACT.Copy,
+                        scale=one_minus_mix[:, PACK * g + t : PACK * g + t + 1],
+                    )
+            for u in range(2):
+                for e in range(2):
+                    t = 2 * u + e
+                    nc.vector.scalar_tensor_tensor(
+                        out=xr_rows[:, t, :],
+                        in0=x_vals[:, :, u, e],
+                        scalar=mix[:, PACK * g + t : PACK * g + t + 1],
+                        in1=sx_part[:, t, :],
+                        op0=ALU.mult,
+                        op1=ALU.add,
+                    )
+            xr_group = work.tile([P, B, PACK], BF16, align_bytes=64)
+            nc.vector.tensor_copy(out=xr_group[:], in_=xr_rows[:].rearrange("p t j -> p j t"))
+            xr_grouped[g] = xr_group
+            if g > 0:
+                quantise_pass(xr_grouped[g - 1], xr_codes, xr_scales, g - 1)
+        quantise_pass(xr_grouped[PASSES - 1], xr_codes, xr_scales, PASSES - 1)
+
+        log_den = keep.tile([P, PASSES, B, PACK], F32)
+        for g in range(PASSES):
+            den_bank = transpose_pass(den_raw, g)
+            nc.scalar.activation(out=by_pairs(log_den[:, g]), in_=values(den_bank), func=ACT.Ln)
+        ratio = keep.tile([P, PASSES, B, PACK], F32)
+
+        def form_ratio(g):
+            inv_den = work.tile([P, B, PACK], F32)
+            nc.scalar.activation(out=inv_den[:], in_=log_den[:, g], func=ACT.Exp, scale=-1.0)
+            num_bank = transpose_pass(num_raw, g)
+            nc.vector.tensor_tensor(
+                out=by_pairs(ratio[:, g]), in0=values(num_bank), in1=by_pairs(inv_den[:]), op=ALU.mult
+            )
+
+        slab_grouped = {}
+        slab_codes = {}
+        slab_scales = {}
+
+        def transpose_slab(i):
+            grouped = stage.tile([P, PASSES, SLAB, PACK], BF16, align_bytes=64)
+            grouped_words = grouped[:].bitcast(F32)
+            for g in range(PASSES):
+                bank = transpose_pass(slab_raw[i], g)
+                pairs = bank[:].rearrange("p u j -> p j u")
+                if g < PASSES - 1:
+                    nc.scalar.copy(out=grouped_words[:, g], in_=pairs)
+                else:
+                    nc.vector.tensor_copy(out=grouped_words[:, g], in_=pairs)
+            slab_grouped[i] = grouped
+            if i + RAW_BUFS < 2 * SLABS:
+                load_slab(i + RAW_BUFS)
+
+        def quantise_slab(i):
+            w_codes = quantised.tile([P, PASSES, SLAB], U32, align_bytes=64)
+            w_scales = quantised.tile([P, PASSES, SLAB], U8, align_bytes=64)
+            nc.vector.quantize_mx(
+                out=w_codes[:].rearrange("p g j -> p (g j)").bitcast(FP8X4),
+                scales=w_scales[:].rearrange("p g j -> p (g j)"),
+                in_=slab_grouped[i][:].rearrange("p g j t -> p (g j t)"),
+            )
+            slab_codes[i] = w_codes
+            slab_scales[i] = w_scales
+
+        gates = {}
+        h_grouped = {}
+
+        def receptance_slab(c):
+            z = sums.tile([P, 2, B], F32, tag="sum")
+            for s in range(2):
+                for g in range(PASSES):
+                    nc.tensor.matmul_mx(
+                        out=z[:, s, :],
+                        lhsT=slab_codes[c][:, g, s * P : (s + 1) * P].bitcast(FP8X4),
+                        lhsT_scale=slab_scales[c][:, g, s * P : (s + 1) * P],
+                        rhs=xr_codes[:, g, :].bitcast(FP8X4),
+                        rhs_scale=xr_scales[:, g, :],
+                        start=(g == 0),
+                        stop=(g == PASSES - 1),
+                    )
+            g2, u = divmod(c, 2)
+            if u == 0:
+                gate = work.tile([P, PACK, B], F32)
+                gates[g2] = gate
+            nc.scalar.activation(
+                out=gates[g2][:, 2 * u : 2 * u + 2, :], in_=z[:], func=ACT.Relu, scale=1.0 / 6.0, bias=0.5
+            )
+            if u == 1:
+                h_group = work.tile([P, B, PACK], BF16, align_bytes=64)
+                nc.vector.scalar_tensor_tensor(
+                    out=h_group[:],
+                    in0=gates[g2][:].rearrange("p t j -> p j t"),
+                    scalar=1.0,
+                    in1=ratio[:, g2],
+                    op0=ALU.min,
+                    op1=ALU.mult,
+                )
+                h_grouped[g2] = h_group
+
+        out_rows = out.rearrange("(p s) n -> p s n", s=2)
+
+        def output_slab(c):
+            o = sums.tile([P, 2, SLAB], F32, tag="sum")
+            for s in range(2):
+                for g in range(PASSES):
+                    nc.tensor.matmul_mx(
+                        out=o[:, s, :],
+                        lhsT=h_codes[:, g, s * P : (s + 1) * P].bitcast(FP8X4),
+                        lhsT_scale=h_scales[:, g, s * P : (s + 1) * P],
+                        rhs=slab_codes[SLABS + c][:, g, :].bitcast(FP8X4),
+                        rhs_scale=slab_scales[SLABS + c][:, g, :],
+                        start=(g == 0),
+                        stop=(g == PASSES - 1),
+                    )
+            o_sb = work.tile([P, 2, P, 2], F32)
+            nc.scalar.copy(out=o_sb[:], in_=o[:].rearrange("p s (s2 r2) -> p s r2 s2", s2=2))
+            nc.sync.dma_start(
+                out=out_rows[:, :, c * SLAB : (c + 1) * SLAB],
+                in_=o_sb[:].rearrange("p s r2 s2 -> p s (r2 s2)"),
+            )
+
+        for i in range(AHEAD):
+            transpose_slab(i)
+        quantise_slab(0)
+        for i in range(2 * SLABS):
+            if i < PASSES:
+                form_ratio(i)
+            if i + AHEAD < 2 * SLABS:
+                transpose_slab(i + AHEAD)
+            if i % 2 == 0 and 2 <= i <= SLABS:
+                quantise_pass(h_grouped[i // 2 - 1], h_codes, h_scales, i // 2 - 1)
+            if i + 1 < 2 * SLABS:
+                quantise_slab(i + 1)
+            if i < SLABS:
+                receptance_slab(i)
+            else:
+                output_slab(i - SLABS)

@@ -19,7 +19,7 @@ PASSES = K // (P * PACK)
 SLAB = 2 * P
 SLABS = K // SLAB
 RAW_BUFS = 8
-AHEAD = 2
+AHEAD = 3
 
 FLOPS = 2 * 2 * B * K * K
 
@@ -33,7 +33,7 @@ def tile_rwkv_timemix_for_quant_pb_kernel(
         acts = ctx.enter_context(tc.tile_pool(name="acts", bufs=1))
         raw = ctx.enter_context(tc.tile_pool(name="raw", bufs=RAW_BUFS))
         stage = ctx.enter_context(tc.tile_pool(name="stage", bufs=3))
-        quantised = ctx.enter_context(tc.tile_pool(name="quantised", bufs=AHEAD + 2))
+        quantised = ctx.enter_context(tc.tile_pool(name="quantised", bufs=AHEAD + 1))
         keep = ctx.enter_context(tc.tile_pool(name="keep", bufs=1))
         work = ctx.enter_context(tc.tile_pool(name="work", bufs=2))
         tbanks = ctx.enter_context(tc.psum_pool(name="tbanks", bufs=6))
@@ -42,6 +42,11 @@ def tile_rwkv_timemix_for_quant_pb_kernel(
 
         ident = consts.tile([P, P], F32)
         make_identity(nc, ident[:])
+
+        one = consts.tile([P, 1], F32)
+        nc.vector.memset(one[:], 1.0)
+        zero = consts.tile([P, 1], F32)
+        nc.scalar.activation(out=zero[:], in_=one[:], func=ACT.Ln)
 
         mix_rows = consts.tile([P, 2 * P], BF16)
         nc.vector.memset(mix_rows[:], 0.0)
@@ -53,10 +58,16 @@ def tile_rwkv_timemix_for_quant_pb_kernel(
         def load_rows(dst, rows):
             nc.sync.dma_start(out=dst[:], in_=rows.rearrange("(p s) k -> p s k", s=2))
 
-        x_raw = acts.tile([P, 2, K], BF16)
-        load_rows(x_raw, x)
-        sx_raw = acts.tile([P, 2, K], BF16)
-        load_rows(sx_raw, state_x)
+        x_lo = acts.tile([P, 2, K // 2], BF16)
+        load_rows(x_lo, x[:, 0 : K // 2])
+        sx_lo = acts.tile([P, 2, K // 2], BF16)
+        load_rows(sx_lo, state_x[:, 0 : K // 2])
+        x_hi = acts.tile([P, 2, K // 2], BF16)
+        load_rows(x_hi, x[:, K // 2 : K])
+        sx_hi = acts.tile([P, 2, K // 2], BF16)
+        load_rows(sx_hi, state_x[:, K // 2 : K])
+        x_halves = [x_lo, x_hi]
+        sx_halves = [sx_lo, sx_hi]
         den_raw = acts.tile([P, 2, K], BF16)
         load_rows(den_raw, wkv_den)
         num_raw = acts.tile([P, 2, K], BF16)
@@ -112,11 +123,11 @@ def tile_rwkv_timemix_for_quant_pb_kernel(
                 in_=grouped[:].rearrange("p j t -> p (j t)"),
             )
 
-        x_banks = [transpose_pass(x_raw, g) for g in range(PASSES)]
         xr_grouped = {}
         for g in range(PASSES):
-            x_vals = values(x_banks[g])
-            sx_vals = values(transpose_pass(sx_raw, g))
+            half, g_in_half = divmod(g, PASSES // 2)
+            x_vals = values(transpose_pass(x_halves[half], g_in_half))
+            sx_vals = values(transpose_pass(sx_halves[half], g_in_half))
             sx_part = work.tile([P, PACK, B], F32)
             xr_rows = work.tile([P, PACK, B], BF16)
             for u in range(2):
@@ -248,7 +259,8 @@ def tile_rwkv_timemix_for_quant_pb_kernel(
 
         for i in range(AHEAD):
             transpose_slab(i)
-        quantise_slab(0)
+        for i in range(AHEAD - 1):
+            quantise_slab(i)
         for i in range(2 * SLABS):
             if i < PASSES:
                 form_ratio(i)
@@ -256,8 +268,8 @@ def tile_rwkv_timemix_for_quant_pb_kernel(
                 transpose_slab(i + AHEAD)
             if i % 2 == 0 and 2 <= i <= SLABS:
                 quantise_pass(h_grouped[i // 2 - 1], h_codes, h_scales, i // 2 - 1)
-            if i + 1 < 2 * SLABS:
-                quantise_slab(i + 1)
+            if i + AHEAD - 1 < 2 * SLABS:
+                quantise_slab(i + AHEAD - 1)
             if i < SLABS:
                 receptance_slab(i)
             else:

@@ -45,8 +45,8 @@ def tile_rwkv_timemix_for_quant_pb_kernel(
 
         one = consts.tile([P, 1], F32)
         nc.vector.memset(one[:], 1.0)
-        zero = consts.tile([P, 1], F32)
-        nc.scalar.activation(out=zero[:], in_=one[:], func=ACT.Ln)
+        warm = consts.tile([P, 1], F32)
+        nc.scalar.activation(out=warm[:], in_=one[:], func=ACT.Abs_reciprocal_sqrt)
 
         mix_rows = consts.tile([P, 2 * P], BF16)
         nc.vector.memset(mix_rows[:], 0.0)
@@ -157,15 +157,17 @@ def tile_rwkv_timemix_for_quant_pb_kernel(
                 quantise_pass(xr_grouped[g - 1], xr_codes, xr_scales, g - 1)
         quantise_pass(xr_grouped[PASSES - 1], xr_codes, xr_scales, PASSES - 1)
 
-        log_den = keep.tile([P, PASSES, B, PACK], F32)
+        root_inv_den = keep.tile([P, PASSES, B, PACK], F32)
         for g in range(PASSES):
             den_bank = transpose_pass(den_raw, g)
-            nc.scalar.activation(out=by_pairs(log_den[:, g]), in_=values(den_bank), func=ACT.Ln)
+            nc.scalar.activation(
+                out=by_pairs(root_inv_den[:, g]), in_=values(den_bank), func=ACT.Abs_reciprocal_sqrt
+            )
         ratio = keep.tile([P, PASSES, B, PACK], F32)
 
         def form_ratio(g):
             inv_den = work.tile([P, B, PACK], F32)
-            nc.scalar.activation(out=inv_den[:], in_=log_den[:, g], func=ACT.Exp, scale=-1.0)
+            nc.scalar.activation(out=inv_den[:], in_=root_inv_den[:, g], func=ACT.Square)
             num_bank = transpose_pass(num_raw, g)
             nc.vector.tensor_tensor(
                 out=by_pairs(ratio[:, g]), in0=values(num_bank), in1=by_pairs(inv_den[:]), op=ALU.mult
@@ -175,16 +177,16 @@ def tile_rwkv_timemix_for_quant_pb_kernel(
         slab_codes = {}
         slab_scales = {}
 
-        def transpose_slab(i):
+        def transpose_slab(i, vector_banks):
             grouped = stage.tile([P, PASSES, SLAB, PACK], BF16, align_bytes=64)
             grouped_words = grouped[:].bitcast(F32)
             for g in range(PASSES):
                 bank = transpose_pass(slab_raw[i], g)
                 pairs = bank[:].rearrange("p u j -> p j u")
-                if g < PASSES - 1:
-                    nc.scalar.copy(out=grouped_words[:, g], in_=pairs)
-                else:
+                if g in vector_banks:
                     nc.vector.tensor_copy(out=grouped_words[:, g], in_=pairs)
+                else:
+                    nc.scalar.copy(out=grouped_words[:, g], in_=pairs)
             slab_grouped[i] = grouped
             if i + RAW_BUFS < 2 * SLABS:
                 load_slab(i + RAW_BUFS)
@@ -258,14 +260,14 @@ def tile_rwkv_timemix_for_quant_pb_kernel(
             )
 
         for i in range(AHEAD):
-            transpose_slab(i)
+            transpose_slab(i, (1, 3))
         for i in range(AHEAD - 1):
             quantise_slab(i)
         for i in range(2 * SLABS):
             if i < PASSES:
                 form_ratio(i)
             if i + AHEAD < 2 * SLABS:
-                transpose_slab(i + AHEAD)
+                transpose_slab(i + AHEAD, (3,))
             if i % 2 == 0 and 2 <= i <= SLABS:
                 quantise_pass(h_grouped[i // 2 - 1], h_codes, h_scales, i // 2 - 1)
             if i + AHEAD - 1 < 2 * SLABS:

from contextlib import ExitStack

import concourse.mybir as mybir
from concourse.masks import make_identity

F32 = mybir.dt.float32
BF16 = mybir.dt.bfloat16
U32 = mybir.dt.uint32
U8 = mybir.dt.uint8
FP8X4 = mybir.dt.float8_e4m3fn_x4
ACT = mybir.ActivationFunctionType
ALU = mybir.AluOpType

P = 128
B = 256
K = 2048
PACK = 4
PASSES = K // (P * PACK)
SLAB = 2 * P
SLABS = K // SLAB
RAW_BUFS = 8
AHEAD = 3

FLOPS = 2 * 2 * B * K * K


def tile_rwkv_timemix_for_quant_pb_kernel(
    tc, x, state_x, time_mix_r, W_receptance, wkv_num, wkv_den, W_output, out
):
    nc = tc.nc
    with ExitStack() as ctx:
        consts = ctx.enter_context(tc.tile_pool(name="consts", bufs=1))
        acts = ctx.enter_context(tc.tile_pool(name="acts", bufs=1))
        raw = ctx.enter_context(tc.tile_pool(name="raw", bufs=RAW_BUFS))
        stage = ctx.enter_context(tc.tile_pool(name="stage", bufs=3))
        quantised = ctx.enter_context(tc.tile_pool(name="quantised", bufs=AHEAD + 1))
        keep = ctx.enter_context(tc.tile_pool(name="keep", bufs=1))
        work = ctx.enter_context(tc.tile_pool(name="work", bufs=2))
        tbanks = ctx.enter_context(tc.psum_pool(name="tbanks", bufs=6))
        sums = ctx.enter_context(tc.psum_pool(name="sums", bufs=2))
        ctx.enter_context(tc.manual_schedule())

        ident = consts.tile([P, P], F32)
        make_identity(nc, ident[:])

        one = consts.tile([P, 1], F32)
        nc.vector.memset(one[:], 1.0)
        warm = consts.tile([P, 1], F32)
        nc.scalar.activation(out=warm[:], in_=one[:], func=ACT.Abs_reciprocal_sqrt)

        mix_rows = consts.tile([P, 2 * P], BF16)
        nc.vector.memset(mix_rows[:], 0.0)
        nc.sync.dma_start(
            out=mix_rows[0 : 2 * PASSES, :],
            in_=time_mix_r.rearrange("o (w c) -> (o w) c", w=2 * PASSES),
        )

        def load_rows(dst, rows):
            nc.sync.dma_start(out=dst[:], in_=rows.rearrange("(p s) k -> p s k", s=2))

        x_lo = acts.tile([P, 2, K // 2], BF16)
        load_rows(x_lo, x[:, 0 : K // 2])
        sx_lo = acts.tile([P, 2, K // 2], BF16)
        load_rows(sx_lo, state_x[:, 0 : K // 2])
        x_hi = acts.tile([P, 2, K // 2], BF16)
        load_rows(x_hi, x[:, K // 2 : K])
        sx_hi = acts.tile([P, 2, K // 2], BF16)
        load_rows(sx_hi, state_x[:, K // 2 : K])
        x_halves = [x_lo, x_hi]
        sx_halves = [sx_lo, sx_hi]
        den_raw = acts.tile([P, 2, K], BF16)
        load_rows(den_raw, wkv_den)
        num_raw = acts.tile([P, 2, K], BF16)
        load_rows(num_raw, wkv_num)

        slab_raw = {}

        def load_slab(i):
            w_raw = raw.tile([P, 2, K], BF16)
            weight = W_receptance if i < SLABS else W_output
            c = i % SLABS
            load_rows(w_raw, weight[c * SLAB : (c + 1) * SLAB, :])
            slab_raw[i] = w_raw

        for i in range(RAW_BUFS):
            load_slab(i)

        def transpose_pass(src, g):
            words = src[:].bitcast(F32)
            bank = tbanks.tile([P, 2, SLAB], F32)
            for u in range(2):
                w = 2 * g + u
                for s in range(2):
                    nc.tensor.transpose(
                        bank[:, u, s * P : (s + 1) * P], words[:, s, w * P : (w + 1) * P], ident[:]
                    )
            return bank

        def values(bank):
            return bank[:].bitcast(BF16).rearrange("p u (j e) -> p j u e", e=2)

        def by_pairs(ap):
            return ap.rearrange("p j (u e) -> p j u e", e=2)

        mix_bank = tbanks.tile([P, 2, SLAB], F32, tag="bank")
        nc.tensor.transpose(mix_bank[:, 0, 0:P], mix_rows[:].bitcast(F32), ident[:])
        mix = consts.tile([P, PACK * PASSES], F32)
        nc.vector.tensor_copy(out=mix[:], in_=mix_bank[:, 0, 0 : 2 * PASSES].bitcast(BF16))
        one_minus_mix = consts.tile([P, PACK * PASSES], F32)
        nc.vector.tensor_scalar(
            out=one_minus_mix[:], in0=mix[:], scalar1=-1.0, scalar2=1.0, op0=ALU.mult, op1=ALU.add
        )

        xr_codes = keep.tile([P, PASSES, B], U32, align_bytes=64)
        xr_scales = keep.tile([P, PASSES, B], U8, align_bytes=64)
        h_codes = keep.tile([P, PASSES, B], U32, align_bytes=64)
        h_scales = keep.tile([P, PASSES, B], U8, align_bytes=64)

        def quantise_pass(grouped, codes, scales, g):
            nc.vector.quantize_mx(
                out=codes[:, g, :].bitcast(FP8X4),
                scales=scales[:, g, :],
                in_=grouped[:].rearrange("p j t -> p (j t)"),
            )

        xr_grouped = {}
        for g in range(PASSES):
            half, g_in_half = divmod(g, PASSES // 2)
            x_vals = values(transpose_pass(x_halves[half], g_in_half))
            sx_vals = values(transpose_pass(sx_halves[half], g_in_half))
            sx_part = work.tile([P, PACK, B], F32)
            xr_rows = work.tile([P, PACK, B], BF16)
            for u in range(2):
                for e in range(2):
                    t = 2 * u + e
                    nc.scalar.activation(
                        out=sx_part[:, t, :],
                        in_=sx_vals[:, :, u, e],
                        func=ACT.Copy,
                        scale=one_minus_mix[:, PACK * g + t : PACK * g + t + 1],
                    )
            for u in range(2):
                for e in range(2):
                    t = 2 * u + e
                    nc.vector.scalar_tensor_tensor(
                        out=xr_rows[:, t, :],
                        in0=x_vals[:, :, u, e],
                        scalar=mix[:, PACK * g + t : PACK * g + t + 1],
                        in1=sx_part[:, t, :],
                        op0=ALU.mult,
                        op1=ALU.add,
                    )
            xr_group = work.tile([P, B, PACK], BF16, align_bytes=64)
            nc.vector.tensor_copy(out=xr_group[:], in_=xr_rows[:].rearrange("p t j -> p j t"))
            xr_grouped[g] = xr_group
            if g > 0:
                quantise_pass(xr_grouped[g - 1], xr_codes, xr_scales, g - 1)
        quantise_pass(xr_grouped[PASSES - 1], xr_codes, xr_scales, PASSES - 1)

        root_inv_den = keep.tile([P, PASSES, B, PACK], F32)
        for g in range(PASSES):
            den_bank = transpose_pass(den_raw, g)
            nc.scalar.activation(
                out=by_pairs(root_inv_den[:, g]), in_=values(den_bank), func=ACT.Abs_reciprocal_sqrt
            )
        ratio = keep.tile([P, PASSES, B, PACK], F32)

        def form_ratio(g):
            inv_den = work.tile([P, B, PACK], F32)
            nc.scalar.activation(out=inv_den[:], in_=root_inv_den[:, g], func=ACT.Square)
            num_bank = transpose_pass(num_raw, g)
            nc.vector.tensor_tensor(
                out=by_pairs(ratio[:, g]), in0=values(num_bank), in1=by_pairs(inv_den[:]), op=ALU.mult
            )

        slab_grouped = {}
        slab_codes = {}
        slab_scales = {}

        def transpose_slab(i, vector_banks):
            grouped = stage.tile([P, PASSES, SLAB, PACK], BF16, align_bytes=64)
            grouped_words = grouped[:].bitcast(F32)
            for g in range(PASSES):
                bank = transpose_pass(slab_raw[i], g)
                pairs = bank[:].rearrange("p u j -> p j u")
                if g in vector_banks:
                    nc.vector.tensor_copy(out=grouped_words[:, g], in_=pairs)
                else:
                    nc.scalar.copy(out=grouped_words[:, g], in_=pairs)
            slab_grouped[i] = grouped
            if i + RAW_BUFS < 2 * SLABS:
                load_slab(i + RAW_BUFS)

        def quantise_slab(i):
            w_codes = quantised.tile([P, PASSES, SLAB], U32, align_bytes=64)
            w_scales = quantised.tile([P, PASSES, SLAB], U8, align_bytes=64)
            nc.vector.quantize_mx(
                out=w_codes[:].rearrange("p g j -> p (g j)").bitcast(FP8X4),
                scales=w_scales[:].rearrange("p g j -> p (g j)"),
                in_=slab_grouped[i][:].rearrange("p g j t -> p (g j t)"),
            )
            slab_codes[i] = w_codes
            slab_scales[i] = w_scales

        gates = {}
        h_grouped = {}

        def receptance_slab(c):
            z = sums.tile([P, 2, B], F32, tag="sum")
            for s in range(2):
                for g in range(PASSES):
                    nc.tensor.matmul_mx(
                        out=z[:, s, :],
                        lhsT=slab_codes[c][:, g, s * P : (s + 1) * P].bitcast(FP8X4),
                        lhsT_scale=slab_scales[c][:, g, s * P : (s + 1) * P],
                        rhs=xr_codes[:, g, :].bitcast(FP8X4),
                        rhs_scale=xr_scales[:, g, :],
                        start=(g == 0),
                        stop=(g == PASSES - 1),
                    )
            g2, u = divmod(c, 2)
            if u == 0:
                gate = work.tile([P, PACK, B], F32)
                gates[g2] = gate
            nc.scalar.activation(
                out=gates[g2][:, 2 * u : 2 * u + 2, :], in_=z[:], func=ACT.Relu, scale=1.0 / 6.0, bias=0.5
            )
            if u == 1:
                h_group = work.tile([P, B, PACK], BF16, align_bytes=64)
                nc.vector.scalar_tensor_tensor(
                    out=h_group[:],
                    in0=gates[g2][:].rearrange("p t j -> p j t"),
                    scalar=1.0,
                    in1=ratio[:, g2],
                    op0=ALU.min,
                    op1=ALU.mult,
                )
                h_grouped[g2] = h_group

        out_rows = out.rearrange("(p s) n -> p s n", s=2)

        def output_slab(c):
            o = sums.tile([P, 2, SLAB], F32, tag="sum")
            for s in range(2):
                for g in range(PASSES):
                    nc.tensor.matmul_mx(
                        out=o[:, s, :],
                        lhsT=h_codes[:, g, s * P : (s + 1) * P].bitcast(FP8X4),
                        lhsT_scale=h_scales[:, g, s * P : (s + 1) * P],
                        rhs=slab_codes[SLABS + c][:, g, :].bitcast(FP8X4),
                        rhs_scale=slab_scales[SLABS + c][:, g, :],
                        start=(g == 0),
                        stop=(g == PASSES - 1),
                    )
            o_sb = work.tile([P, 2, P, 2], F32)
            nc.scalar.copy(out=o_sb[:], in_=o[:].rearrange("p s (s2 r2) -> p s r2 s2", s2=2))
            nc.sync.dma_start(
                out=out_rows[:, :, c * SLAB : (c + 1) * SLAB],
                in_=o_sb[:].rearrange("p s r2 s2 -> p s (r2 s2)"),
            )

        for i in range(AHEAD):
            transpose_slab(i, (1, 3))
        for i in range(AHEAD - 1):
            quantise_slab(i)
        for i in range(2 * SLABS):
            if i < PASSES:
                form_ratio(i)
            if i + AHEAD < 2 * SLABS:
                transpose_slab(i + AHEAD, (3,))
            if i % 2 == 0 and 2 <= i <= SLABS:
                quantise_pass(h_grouped[i // 2 - 1], h_codes, h_scales, i // 2 - 1)
            if i + AHEAD - 1 < 2 * SLABS:
                quantise_slab(i + AHEAD - 1)
            if i < SLABS:
                receptance_slab(i)
            else:
                output_slab(i - SLABS)
